import numpy as np
import ml_dtypes

BF16 = ml_dtypes.bfloat16


def bf(x):
    return np.asarray(x, np.float32).astype(BF16)


def f32(x):
    return np.asarray(x, np.float32)


def f64(x):
    return np.asarray(x).astype(np.float64)


def striped(idx):
    return np.tile(idx.reshape(-1, 16).T, (8, 1))


C, S, N = 128, 1024, 1024
EPS = 1e-5


def setup_inputs():
    return {"tok_emb": f32(np.random.standard_normal((C, S))), "pos_emb": f32(np.random.standard_normal((C, N))), "gain": f32(1.0 + 0.1 * np.random.standard_normal((C, 1))), "beta": f32(0.1 * np.random.standard_normal((C, 1))), "wl": bf(np.random.standard_normal((C, S)) / np.sqrt(C)), "bl": f32(0.1 * np.random.standard_normal((S, 1))), "offs": striped(np.random.permutation(np.tile(np.arange(S), 2))[:N])}


def reference(tok_emb, pos_emb, gain, beta, wl, bl, offs):
    idx = offs[:16].T.reshape(-1)
    x = f64(tok_emb)[:, idx] + f64(pos_emb)
    m = x.mean(axis=0, keepdims=True)
    d = x - m
    var = (d * d).mean(axis=0, keepdims=True)
    y = d / np.sqrt(var + EPS) * f64(gain) + f64(beta)
    return f64(wl).T @ y + f64(bl)

@@ -1,0 +1,89 @@
+import concourse.mybir as mybir
+from concourse.masks import make_identity
+
+F32 = mybir.dt.float32
+BF16 = mybir.dt.bfloat16
+U16 = mybir.dt.uint16
+ALU = mybir.AluOpType
+ACT = mybir.ActivationFunctionType
+
+CHANNELS = 128
+WORDS = 1024
+TOKENS = 1024
+EPS = 1e-5
+CHUNK = 512
+CHUNKS = TOKENS // CHUNK
+BLOCKS = WORDS // 128
+
+FLOPS = 2 * CHANNELS * WORDS * TOKENS
+
+
+def tile_main_kernel(tc, tok_emb, pos_emb, gain, beta, wl, bl, offs, out):
+    nc = tc.nc
+    bl_by_block = bl.rearrange("(p b) o -> p (b o)", b=BLOCKS)
+    out_by_block = out.rearrange("(p b) j -> p b j", b=BLOCKS)
+
+    with (
+        tc.tile_pool(name="held", bufs=1) as held,
+        tc.tile_pool(name="norm", bufs=CHUNKS) as norm,
+        tc.tile_pool(name="staged", bufs=CHUNKS * BLOCKS) as staged,
+        tc.psum_pool(name="stats", bufs=CHUNKS) as stats,
+        tc.psum_pool(name="banks", bufs=4) as banks,
+    ):
+        offsets = held.tile([CHANNELS, TOKENS // 16], U16, name="offsets")
+        nc.sync.dma_start(offsets[:], offs)
+        table = held.tile([CHANNELS, WORDS], F32, name="table")
+        nc.sync.dma_start(table[:], tok_emb)
+        positions = []
+        for k in range(CHUNKS):
+            pos = norm.tile([CHANNELS, CHUNK], F32, name="pos")
+            nc.sync.dma_start(pos[:], pos_emb[:, k * CHUNK : (k + 1) * CHUNK])
+            positions.append(pos)
+        weights = held.tile([CHANNELS, WORDS], BF16, name="weights")
+        nc.sync.dma_start(weights[:], wl)
+        weights_by_block = weights[:].rearrange("c (p b) -> c b p", b=BLOCKS)
+        gain_col = held.tile([CHANNELS, 1], F32, name="gain_col")
+        nc.scalar.dma_start(gain_col[:], gain)
+        beta_col = held.tile([CHANNELS, 1], F32, name="beta_col")
+        nc.scalar.dma_start(beta_col[:], beta)
+        bias = held.tile([128, BLOCKS], F32, name="bias")
+        nc.scalar.dma_start(bias[:], bl_by_block)
+
+        identity = held.tile([CHANNELS, CHANNELS], F32, name="identity")
+        make_identity(nc, identity[:])
+        center = held.tile([CHANNELS, CHANNELS], F32, name="center")
+        nc.vector.tensor_scalar_add(center[:], identity[:], -1.0 / CHANNELS)
+        average = held.tile([CHANNELS, CHANNELS], F32, name="average")
+        nc.vector.memset(average[:], 1.0 / CHANNELS)
+        eps_col = held.tile([CHANNELS, 1], F32, name="eps_col")
+        nc.vector.memset(eps_col[:], EPS)
+
+        normed = []
+        for k in range(CHUNKS):
+            piece = offsets[:, k * (CHUNK // 16) : (k + 1) * (CHUNK // 16)]
+            x = norm.tile([CHANNELS, CHUNK], F32, name="x")
+            nc.vector.tensor_tensor(x[:], table[:].indirect(piece), positions[k][:], ALU.add)
+            d = stats.tile([CHANNELS, CHUNK], F32, name="d")
+            nc.tensor.matmul(d[:], center[:], x[:], start=True, stop=True)
+            squares = norm.tile([CHANNELS, CHUNK], F32, name="squares")
+            nc.scalar.activation(squares[:], d[:], ACT.Square)
+            var = stats.tile([CHANNELS, CHUNK], F32, name="var")
+            nc.tensor.matmul(var[:], average[:], squares[:], start=True, stop=True)
+            rstd = norm.tile([CHANNELS, CHUNK], F32, name="rstd")
+            nc.scalar.activation(rstd[:], var[:], ACT.Abs_reciprocal_sqrt, bias=eps_col[:])
+            scaled = norm.tile([CHANNELS, CHUNK], F32, name="scaled")
+            nc.vector.tensor_tensor(scaled[:], d[:], rstd[:], ALU.mult)
+            y = norm.tile([CHANNELS, CHUNK], BF16, name="y")
+            nc.scalar.activation(y[:], scaled[:], ACT.Identity, bias=beta_col[:], scale=gain_col[:])
+            normed.append(y)
+
+        for k in range(CHUNKS):
+            for b in range(BLOCKS):
+                logits = banks.tile([128, CHUNK], F32, name="logits")
+                nc.tensor.matmul(logits[:], weights_by_block[:, b, :], normed[k][:], start=True, stop=True)
+                result = staged.tile([128, CHUNK], F32, name="result")
+                if b % 2 == 0:
+                    nc.scalar.activation(result[:], logits[:], ACT.Identity, bias=bias[:, b : b + 1])
+                else:
+                    nc.vector.tensor_scalar_add(result[:], logits[:], bias[:, b : b + 1])
+                nc.sync.dma_start(out_by_block[:, b, k * CHUNK : (k + 1) * CHUNK], result[:])

@@ -11,23 +11,25 @@ CHANNELS = 128
 WORDS = 1024
 TOKENS = 1024
 EPS = 1e-5
-CHUNK = 512
-CHUNKS = TOKENS // CHUNK
+PIECES = (256, 256, 256, 256)
 BLOCKS = WORDS // 128
+GROUP = 4
 
 FLOPS = 2 * CHANNELS * WORDS * TOKENS
+
+assert sum(PIECES) == TOKENS
 
 
 def tile_main_kernel(tc, tok_emb, pos_emb, gain, beta, wl, bl, offs, out):
     nc = tc.nc
     bl_by_block = bl.rearrange("(p b) o -> p (b o)", b=BLOCKS)
     out_by_block = out.rearrange("(p b) j -> p b j", b=BLOCKS)
+    starts = [sum(PIECES[:k]) for k in range(len(PIECES))]
 
     with (
         tc.tile_pool(name="held", bufs=1) as held,
-        tc.tile_pool(name="norm", bufs=CHUNKS) as norm,
-        tc.tile_pool(name="staged", bufs=CHUNKS * BLOCKS) as staged,
-        tc.psum_pool(name="stats", bufs=CHUNKS) as stats,
+        tc.tile_pool(name="work", bufs=len(PIECES)) as work,
+        tc.psum_pool(name="stats", bufs=4) as stats,
         tc.psum_pool(name="banks", bufs=4) as banks,
     ):
         offsets = held.tile([CHANNELS, TOKENS // 16], U16, name="offsets")
@@ -35,9 +37,9 @@ def tile_main_kernel(tc, tok_emb, pos_emb, gain, beta, wl, bl, offs, out):
         table = held.tile([CHANNELS, WORDS], F32, name="table")
         nc.sync.dma_start(table[:], tok_emb)
         positions = []
-        for k in range(CHUNKS):
-            pos = norm.tile([CHANNELS, CHUNK], F32, name="pos")
-            nc.sync.dma_start(pos[:], pos_emb[:, k * CHUNK : (k + 1) * CHUNK])
+        for first, n in zip(starts, PIECES):
+            pos = work.tile([CHANNELS, n], F32, name="pos")
+            nc.sync.dma_start(pos[:], pos_emb[:, first : first + n])
             positions.append(pos)
         weights = held.tile([CHANNELS, WORDS], BF16, name="weights")
         nc.sync.dma_start(weights[:], wl)
@@ -58,32 +60,36 @@ def tile_main_kernel(tc, tok_emb, pos_emb, gain, beta, wl, bl, offs, out):
         eps_col = held.tile([CHANNELS, 1], F32, name="eps_col")
         nc.vector.memset(eps_col[:], EPS)
 
-        normed = []
-        for k in range(CHUNKS):
-            piece = offsets[:, k * (CHUNK // 16) : (k + 1) * (CHUNK // 16)]
-            x = norm.tile([CHANNELS, CHUNK], F32, name="x")
-            nc.vector.tensor_tensor(x[:], table[:].indirect(piece), positions[k][:], ALU.add)
-            d = stats.tile([CHANNELS, CHUNK], F32, name="d")
-            nc.tensor.matmul(d[:], center[:], x[:], start=True, stop=True)
-            squares = norm.tile([CHANNELS, CHUNK], F32, name="squares")
-            nc.scalar.activation(squares[:], d[:], ACT.Square)
-            var = stats.tile([CHANNELS, CHUNK], F32, name="var")
-            nc.tensor.matmul(var[:], average[:], squares[:], start=True, stop=True)
-            rstd = norm.tile([CHANNELS, CHUNK], F32, name="rstd")
-            nc.scalar.activation(rstd[:], var[:], ACT.Abs_reciprocal_sqrt, bias=eps_col[:])
-            scaled = norm.tile([CHANNELS, CHUNK], F32, name="scaled")
-            nc.vector.tensor_tensor(scaled[:], d[:], rstd[:], ALU.mult)
-            y = norm.tile([CHANNELS, CHUNK], BF16, name="y")
-            nc.scalar.activation(y[:], scaled[:], ACT.Identity, bias=beta_col[:], scale=gain_col[:])
-            normed.append(y)
+        for i in range(8):
+            idle = banks.tile([CHANNELS, CHANNELS], F32, name="logits")
+            nc.tensor.matmul(idle[:], average[:], average[:], start=True, stop=True)
 
-        for k in range(CHUNKS):
+        for k, (first, n) in enumerate(zip(starts, PIECES)):
+            piece = offsets[:, first // 16 : (first + n) // 16]
+            x = work.tile([CHANNELS, n], F32, name="x")
+            nc.vector.tensor_tensor(x[:], table[:].indirect(piece), positions[k][:], ALU.add)
+            stat = stats.tile([CHANNELS, 2 * n], F32, name="stat")
+            d = stat[:, 0:n]
+            var = stat[:, n : 2 * n]
+            nc.tensor.matmul(d, center[:], x[:], start=True, stop=True)
+            squares = work.tile([CHANNELS, n], F32, name="squares")
+            nc.scalar.activation(squares[:], d, ACT.Square)
+            nc.tensor.matmul(var, average[:], squares[:], start=True, stop=True)
+            rstd = work.tile([CHANNELS, n], F32, name="rstd")
+            nc.scalar.activation(rstd[:], var, ACT.Abs_reciprocal_sqrt, bias=eps_col[:])
+            scaled = work.tile([CHANNELS, n], F32, name="scaled")
+            nc.vector.tensor_tensor(scaled[:], d, rstd[:], ALU.mult)
+            y = work.tile([CHANNELS, n], BF16, name="y")
+            nc.vector.tensor_scalar(y[:], scaled[:], gain_col[:], beta_col[:], ALU.mult, ALU.add)
+
+            result = work.tile([128, BLOCKS, n], F32, name="result")
             for b in range(BLOCKS):
-                logits = banks.tile([128, CHUNK], F32, name="logits")
-                nc.tensor.matmul(logits[:], weights_by_block[:, b, :], normed[k][:], start=True, stop=True)
-                result = staged.tile([128, CHUNK], F32, name="result")
+                logits = banks.tile([128, n], F32, name="logits")
+                nc.tensor.matmul(logits[:], weights_by_block[:, b, :], y[:], start=True, stop=True)
                 if b % 2 == 0:
-                    nc.scalar.activation(result[:], logits[:], ACT.Identity, bias=bias[:, b : b + 1])
+                    nc.scalar.activation(result[:, b, :], logits[:], ACT.Identity, bias=bias[:, b : b + 1])
                 else:
-                    nc.vector.tensor_scalar_add(result[:], logits[:], bias[:, b : b + 1])
-                nc.sync.dma_start(out_by_block[:, b, k * CHUNK : (k + 1) * CHUNK], result[:])
+                    nc.vector.tensor_scalar_add(result[:, b, :], logits[:], bias[:, b : b + 1])
+                if (b + 1) % GROUP == 0:
+                    done = slice(b + 1 - GROUP, b + 1)
+                    nc.sync.dma_start(out_by_block[:, done, first : first + n], result[:, done, :])

@@ -11,7 +11,7 @@ CHANNELS = 128
 WORDS = 1024
 TOKENS = 1024
 EPS = 1e-5
-PIECES = (256, 256, 256, 256)
+PIECES = (128, 128, 256, 256, 256)
 BLOCKS = WORDS // 128
 GROUP = 4
 

@@ -11,24 +11,23 @@ CHANNELS = 128
 WORDS = 1024
 TOKENS = 1024
 EPS = 1e-5
-PIECES = (128, 128, 256, 256, 256)
+CHUNK = 256
+SPAN = 512
 BLOCKS = WORDS // 128
-GROUP = 4
 
 FLOPS = 2 * CHANNELS * WORDS * TOKENS
-
-assert sum(PIECES) == TOKENS
 
 
 def tile_main_kernel(tc, tok_emb, pos_emb, gain, beta, wl, bl, offs, out):
     nc = tc.nc
     bl_by_block = bl.rearrange("(p b) o -> p (b o)", b=BLOCKS)
     out_by_block = out.rearrange("(p b) j -> p b j", b=BLOCKS)
-    starts = [sum(PIECES[:k]) for k in range(len(PIECES))]
 
     with (
         tc.tile_pool(name="held", bufs=1) as held,
-        tc.tile_pool(name="work", bufs=len(PIECES)) as work,
+        tc.tile_pool(name="norm", bufs=TOKENS // CHUNK) as norm,
+        tc.tile_pool(name="spans", bufs=TOKENS // SPAN) as spans,
+        tc.tile_pool(name="staged", bufs=(TOKENS // SPAN) * BLOCKS) as staged,
         tc.psum_pool(name="stats", bufs=4) as stats,
         tc.psum_pool(name="banks", bufs=4) as banks,
     ):
@@ -37,9 +36,9 @@ def tile_main_kernel(tc, tok_emb, pos_emb, gain, beta, wl, bl, offs, out):
         table = held.tile([CHANNELS, WORDS], F32, name="table")
         nc.sync.dma_start(table[:], tok_emb)
         positions = []
-        for first, n in zip(starts, PIECES):
-            pos = work.tile([CHANNELS, n], F32, name="pos")
-            nc.sync.dma_start(pos[:], pos_emb[:, first : first + n])
+        for k in range(TOKENS // CHUNK):
+            pos = norm.tile([CHANNELS, CHUNK], F32, name="pos")
+            nc.sync.dma_start(pos[:], pos_emb[:, k * CHUNK : (k + 1) * CHUNK])
             positions.append(pos)
         weights = held.tile([CHANNELS, WORDS], BF16, name="weights")
         nc.sync.dma_start(weights[:], wl)
@@ -64,32 +63,34 @@ def tile_main_kernel(tc, tok_emb, pos_emb, gain, beta, wl, bl, offs, out):
             idle = banks.tile([CHANNELS, CHANNELS], F32, name="logits")
             nc.tensor.matmul(idle[:], average[:], average[:], start=True, stop=True)
 
-        for k, (first, n) in enumerate(zip(starts, PIECES)):
-            piece = offsets[:, first // 16 : (first + n) // 16]
-            x = work.tile([CHANNELS, n], F32, name="x")
-            nc.vector.tensor_tensor(x[:], table[:].indirect(piece), positions[k][:], ALU.add)
-            stat = stats.tile([CHANNELS, 2 * n], F32, name="stat")
-            d = stat[:, 0:n]
-            var = stat[:, n : 2 * n]
-            nc.tensor.matmul(d, center[:], x[:], start=True, stop=True)
-            squares = work.tile([CHANNELS, n], F32, name="squares")
-            nc.scalar.activation(squares[:], d, ACT.Square)
-            nc.tensor.matmul(var, average[:], squares[:], start=True, stop=True)
-            rstd = work.tile([CHANNELS, n], F32, name="rstd")
-            nc.scalar.activation(rstd[:], var, ACT.Abs_reciprocal_sqrt, bias=eps_col[:])
-            scaled = work.tile([CHANNELS, n], F32, name="scaled")
-            nc.vector.tensor_tensor(scaled[:], d, rstd[:], ALU.mult)
-            y = work.tile([CHANNELS, n], BF16, name="y")
-            nc.vector.tensor_scalar(y[:], scaled[:], gain_col[:], beta_col[:], ALU.mult, ALU.add)
+        for s in range(TOKENS // SPAN):
+            y = spans.tile([CHANNELS, SPAN], BF16, name="y")
+            for i in range(SPAN // CHUNK):
+                k = s * (SPAN // CHUNK) + i
+                piece = offsets[:, k * (CHUNK // 16) : (k + 1) * (CHUNK // 16)]
+                x = norm.tile([CHANNELS, CHUNK], F32, name="x")
+                nc.vector.tensor_tensor(x[:], table[:].indirect(piece), positions[k][:], ALU.add)
+                stat = stats.tile([CHANNELS, 2 * CHUNK], F32, name="stat")
+                d = stat[:, 0:CHUNK]
+                var = stat[:, CHUNK : 2 * CHUNK]
+                nc.tensor.matmul(d, center[:], x[:], start=True, stop=True)
+                squares = norm.tile([CHANNELS, CHUNK], F32, name="squares")
+                nc.scalar.activation(squares[:], d, ACT.Square)
+                nc.tensor.matmul(var, average[:], squares[:], start=True, stop=True)
+                rstd = norm.tile([CHANNELS, CHUNK], F32, name="rstd")
+                nc.scalar.activation(rstd[:], var, ACT.Abs_reciprocal_sqrt, bias=eps_col[:])
+                scaled = norm.tile([CHANNELS, CHUNK], F32, name="scaled")
+                nc.vector.tensor_tensor(scaled[:], d, rstd[:], ALU.mult)
+                nc.vector.tensor_scalar(
+                    y[:, i * CHUNK : (i + 1) * CHUNK], scaled[:], gain_col[:], beta_col[:], ALU.mult, ALU.add
+                )
 
-            result = work.tile([128, BLOCKS, n], F32, name="result")
             for b in range(BLOCKS):
-                logits = banks.tile([128, n], F32, name="logits")
+                logits = banks.tile([128, SPAN], F32, name="logits")
                 nc.tensor.matmul(logits[:], weights_by_block[:, b, :], y[:], start=True, stop=True)
+                result = staged.tile([128, SPAN], F32, name="result")
                 if b % 2 == 0:
-                    nc.scalar.activation(result[:, b, :], logits[:], ACT.Identity, bias=bias[:, b : b + 1])
+                    nc.scalar.activation(result[:], logits[:], ACT.Identity, bias=bias[:, b : b + 1])
                 else:
-                    nc.vector.tensor_scalar_add(result[:, b, :], logits[:], bias[:, b : b + 1])
-                if (b + 1) % GROUP == 0:
-                    done = slice(b + 1 - GROUP, b + 1)
-                    nc.sync.dma_start(out_by_block[:, done, first : first + n], result[:, done, :])
+                    nc.vector.tensor_scalar_add(result[:], logits[:], bias[:, b : b + 1])
+                nc.sync.dma_start(out_by_block[:, b, s * SPAN : (s + 1) * SPAN], result[:])

@@ -59,9 +59,11 @@ def tile_main_kernel(tc, tok_emb, pos_emb, gain, beta, wl, bl, offs, out):
         eps_col = held.tile([CHANNELS, 1], F32, name="eps_col")
         nc.vector.memset(eps_col[:], EPS)
 
-        for i in range(8):
-            idle = banks.tile([CHANNELS, CHANNELS], F32, name="logits")
-            nc.tensor.matmul(idle[:], average[:], average[:], start=True, stop=True)
+        spin = held.tile([CHANNELS, SPAN], BF16, name="spin")
+        nc.vector.memset(spin[:], 1.0)
+        for i in range(5):
+            idle = banks.tile([CHANNELS, SPAN], F32, name="logits")
+            nc.tensor.matmul(idle[:], spin[:, 0:CHANNELS], spin[:], start=True, stop=True)
 
         for s in range(TOKENS // SPAN):
             y = spans.tile([CHANNELS, SPAN], BF16, name="y")

@@ -41,7 +41,6 @@ def tile_main_kernel(tc, tok_emb, pos_emb, gain, beta, wl, bl, offs, out):
             nc.sync.dma_start(pos[:], pos_emb[:, k * CHUNK : (k + 1) * CHUNK])
             positions.append(pos)
         weights = held.tile([CHANNELS, WORDS], BF16, name="weights")
-        nc.sync.dma_start(weights[:], wl)
         weights_by_block = weights[:].rearrange("c (p b) -> c b p", b=BLOCKS)
         gain_col = held.tile([CHANNELS, 1], F32, name="gain_col")
         nc.scalar.dma_start(gain_col[:], gain)
@@ -49,6 +48,7 @@ def tile_main_kernel(tc, tok_emb, pos_emb, gain, beta, wl, bl, offs, out):
         nc.scalar.dma_start(beta_col[:], beta)
         bias = held.tile([128, BLOCKS], F32, name="bias")
         nc.scalar.dma_start(bias[:], bl_by_block)
+        nc.scalar.dma_start(weights[:], wl)
 
         identity = held.tile([CHANNELS, CHANNELS], F32, name="identity")
         make_identity(nc, identity[:])
@@ -59,11 +59,9 @@ def tile_main_kernel(tc, tok_emb, pos_emb, gain, beta, wl, bl, offs, out):
         eps_col = held.tile([CHANNELS, 1], F32, name="eps_col")
         nc.vector.memset(eps_col[:], EPS)
 
-        spin = held.tile([CHANNELS, SPAN], BF16, name="spin")
-        nc.vector.memset(spin[:], 1.0)
-        for i in range(5):
-            idle = banks.tile([CHANNELS, SPAN], F32, name="logits")
-            nc.tensor.matmul(idle[:], spin[:, 0:CHANNELS], spin[:], start=True, stop=True)
+        for i in range(8):
+            idle = banks.tile([CHANNELS, CHANNELS], F32, name="logits")
+            nc.tensor.matmul(idle[:], average[:], average[:], start=True, stop=True)
 
         for s in range(TOKENS // SPAN):
             y = spans.tile([CHANNELS, SPAN], BF16, name="y")

@@ -12,7 +12,8 @@ WORDS = 1024
 TOKENS = 1024
 EPS = 1e-5
 CHUNK = 256
-SPAN = 512
+SPANS = (256, 512, 256)
+BANK = 512
 BLOCKS = WORDS // 128
 
 FLOPS = 2 * CHANNELS * WORDS * TOKENS
@@ -26,8 +27,8 @@ def tile_main_kernel(tc, tok_emb, pos_emb, gain, beta, wl, bl, offs, out):
     with (
         tc.tile_pool(name="held", bufs=1) as held,
         tc.tile_pool(name="norm", bufs=TOKENS // CHUNK) as norm,
-        tc.tile_pool(name="spans", bufs=TOKENS // SPAN) as spans,
-        tc.tile_pool(name="staged", bufs=(TOKENS // SPAN) * BLOCKS) as staged,
+        tc.tile_pool(name="summed", bufs=2) as summed,
+        tc.tile_pool(name="staged", bufs=len(SPANS) * BLOCKS) as staged,
         tc.psum_pool(name="stats", bufs=4) as stats,
         tc.psum_pool(name="banks", bufs=4) as banks,
     ):
@@ -63,34 +64,41 @@ def tile_main_kernel(tc, tok_emb, pos_emb, gain, beta, wl, bl, offs, out):
             idle = banks.tile([CHANNELS, CHANNELS], F32, name="logits")
             nc.tensor.matmul(idle[:], average[:], average[:], start=True, stop=True)
 
-        for s in range(TOKENS // SPAN):
-            y = spans.tile([CHANNELS, SPAN], BF16, name="y")
-            for i in range(SPAN // CHUNK):
-                k = s * (SPAN // CHUNK) + i
-                piece = offsets[:, k * (CHUNK // 16) : (k + 1) * (CHUNK // 16)]
-                x = norm.tile([CHANNELS, CHUNK], F32, name="x")
-                nc.vector.tensor_tensor(x[:], table[:].indirect(piece), positions[k][:], ALU.add)
-                stat = stats.tile([CHANNELS, 2 * CHUNK], F32, name="stat")
-                d = stat[:, 0:CHUNK]
-                var = stat[:, CHUNK : 2 * CHUNK]
-                nc.tensor.matmul(d, center[:], x[:], start=True, stop=True)
-                squares = norm.tile([CHANNELS, CHUNK], F32, name="squares")
-                nc.scalar.activation(squares[:], d, ACT.Square)
-                nc.tensor.matmul(var, average[:], squares[:], start=True, stop=True)
-                rstd = norm.tile([CHANNELS, CHUNK], F32, name="rstd")
-                nc.scalar.activation(rstd[:], var, ACT.Abs_reciprocal_sqrt, bias=eps_col[:])
-                scaled = norm.tile([CHANNELS, CHUNK], F32, name="scaled")
-                nc.vector.tensor_tensor(scaled[:], d, rstd[:], ALU.mult)
-                nc.vector.tensor_scalar(
-                    y[:, i * CHUNK : (i + 1) * CHUNK], scaled[:], gain_col[:], beta_col[:], ALU.mult, ALU.add
-                )
+        y = held.tile([CHANNELS, TOKENS], BF16, name="y")
 
+        def normalise(k):
+            piece = offsets[:, k * (CHUNK // 16) : (k + 1) * (CHUNK // 16)]
+            x = summed.tile([CHANNELS, CHUNK], F32, name="x")
+            nc.vector.tensor_tensor(x[:], table[:].indirect(piece), positions[k][:], ALU.add)
+            stat = stats.tile([CHANNELS, 2 * CHUNK], F32, name="stat")
+            d = stat[:, 0:CHUNK]
+            var = stat[:, CHUNK : 2 * CHUNK]
+            nc.tensor.matmul(d, center[:], x[:], start=True, stop=True)
+            squares = norm.tile([CHANNELS, CHUNK], F32, name="squares")
+            nc.scalar.activation(squares[:], d, ACT.Square)
+            nc.tensor.matmul(var, average[:], squares[:], start=True, stop=True)
+            rstd = norm.tile([CHANNELS, CHUNK], F32, name="rstd")
+            nc.scalar.activation(rstd[:], var, ACT.Abs_reciprocal_sqrt, bias=eps_col[:])
+            scaled = norm.tile([CHANNELS, CHUNK], F32, name="scaled")
+            nc.vector.tensor_tensor(scaled[:], d, rstd[:], ALU.mult)
+            nc.vector.tensor_scalar(
+                y[:, k * CHUNK : (k + 1) * CHUNK], scaled[:], gain_col[:], beta_col[:], ALU.mult, ALU.add
+            )
+
+        def project(j, n):
             for b in range(BLOCKS):
-                logits = banks.tile([128, SPAN], F32, name="logits")
-                nc.tensor.matmul(logits[:], weights_by_block[:, b, :], y[:], start=True, stop=True)
-                result = staged.tile([128, SPAN], F32, name="result")
+                logits = banks.tile([128, BANK], F32, name="logits")
+                nc.tensor.matmul(logits[:, 0:n], weights_by_block[:, b, :], y[:, j : j + n], start=True, stop=True)
+                result = staged.tile([128, BANK], F32, name="result")
                 if b % 2 == 0:
-                    nc.scalar.activation(result[:], logits[:], ACT.Identity, bias=bias[:, b : b + 1])
+                    nc.scalar.activation(result[:, 0:n], logits[:, 0:n], ACT.Identity, bias=bias[:, b : b + 1])
                 else:
-                    nc.vector.tensor_scalar_add(result[:], logits[:], bias[:, b : b + 1])
-                nc.sync.dma_start(out_by_block[:, b, s * SPAN : (s + 1) * SPAN], result[:])
+                    nc.vector.tensor_scalar_add(result[:, 0:n], logits[:, 0:n], bias[:, b : b + 1])
+                nc.sync.dma_start(out_by_block[:, b, j : j + n], result[:, 0:n])
+
+        for k in range(TOKENS // CHUNK):
+            normalise(k)
+        first_token = 0
+        for n in SPANS:
+            project(first_token, n)
+            first_token += n

@@ -59,6 +59,8 @@ def tile_main_kernel(tc, tok_emb, pos_emb, gain, beta, wl, bl, offs, out):
         nc.vector.memset(average[:], 1.0 / CHANNELS)
         eps_col = held.tile([CHANNELS, 1], F32, name="eps_col")
         nc.vector.memset(eps_col[:], EPS)
+        primed = held.tile([CHANNELS, 1], F32, name="primed")
+        nc.scalar.activation(primed[:], eps_col[:], ACT.Abs_reciprocal_sqrt)
 
         for i in range(8):
             idle = banks.tile([CHANNELS, CHANNELS], F32, name="logits")

@@ -11,8 +11,9 @@ CHANNELS = 128
 WORDS = 1024
 TOKENS = 1024
 EPS = 1e-5
-CHUNK = 256
-SPANS = (256, 512, 256)
+CHUNKS = (128, 128, 256, 256, 256)
+WIDEST = max(CHUNKS)
+SPANS = (128, 384, 512)
 BANK = 512
 BLOCKS = WORDS // 128
 
@@ -26,7 +27,7 @@ def tile_main_kernel(tc, tok_emb, pos_emb, gain, beta, wl, bl, offs, out):
 
     with (
         tc.tile_pool(name="held", bufs=1) as held,
-        tc.tile_pool(name="norm", bufs=TOKENS // CHUNK) as norm,
+        tc.tile_pool(name="norm", bufs=len(CHUNKS)) as norm,
         tc.tile_pool(name="summed", bufs=2) as summed,
         tc.tile_pool(name="staged", bufs=len(SPANS) * BLOCKS) as staged,
         tc.psum_pool(name="stats", bufs=4) as stats,
@@ -37,10 +38,12 @@ def tile_main_kernel(tc, tok_emb, pos_emb, gain, beta, wl, bl, offs, out):
         table = held.tile([CHANNELS, WORDS], F32, name="table")
         nc.sync.dma_start(table[:], tok_emb)
         positions = []
-        for k in range(TOKENS // CHUNK):
-            pos = norm.tile([CHANNELS, CHUNK], F32, name="pos")
-            nc.sync.dma_start(pos[:], pos_emb[:, k * CHUNK : (k + 1) * CHUNK])
+        first_token = 0
+        for n in CHUNKS:
+            pos = norm.tile([CHANNELS, WIDEST], F32, name="pos")
+            nc.sync.dma_start(pos[:, 0:n], pos_emb[:, first_token : first_token + n])
             positions.append(pos)
+            first_token += n
         weights = held.tile([CHANNELS, WORDS], BF16, name="weights")
         weights_by_block = weights[:].rearrange("c (p b) -> c b p", b=BLOCKS)
         gain_col = held.tile([CHANNELS, 1], F32, name="gain_col")
@@ -68,24 +71,22 @@ def tile_main_kernel(tc, tok_emb, pos_emb, gain, beta, wl, bl, offs, out):
 
         y = held.tile([CHANNELS, TOKENS], BF16, name="y")
 
-        def normalise(k):
-            piece = offsets[:, k * (CHUNK // 16) : (k + 1) * (CHUNK // 16)]
-            x = summed.tile([CHANNELS, CHUNK], F32, name="x")
-            nc.vector.tensor_tensor(x[:], table[:].indirect(piece), positions[k][:], ALU.add)
-            stat = stats.tile([CHANNELS, 2 * CHUNK], F32, name="stat")
-            d = stat[:, 0:CHUNK]
-            var = stat[:, CHUNK : 2 * CHUNK]
-            nc.tensor.matmul(d, center[:], x[:], start=True, stop=True)
-            squares = norm.tile([CHANNELS, CHUNK], F32, name="squares")
-            nc.scalar.activation(squares[:], d, ACT.Square)
-            nc.tensor.matmul(var, average[:], squares[:], start=True, stop=True)
-            rstd = norm.tile([CHANNELS, CHUNK], F32, name="rstd")
-            nc.scalar.activation(rstd[:], var, ACT.Abs_reciprocal_sqrt, bias=eps_col[:])
-            scaled = norm.tile([CHANNELS, CHUNK], F32, name="scaled")
-            nc.vector.tensor_tensor(scaled[:], d, rstd[:], ALU.mult)
-            nc.vector.tensor_scalar(
-                y[:, k * CHUNK : (k + 1) * CHUNK], scaled[:], gain_col[:], beta_col[:], ALU.mult, ALU.add
-            )
+        def normalise(k, j, n):
+            piece = offsets[:, j // 16 : (j + n) // 16]
+            x = summed.tile([CHANNELS, WIDEST], F32, name="x")
+            nc.vector.tensor_tensor(x[:, 0:n], table[:].indirect(piece), positions[k][:, 0:n], ALU.add)
+            stat = stats.tile([CHANNELS, 2 * WIDEST], F32, name="stat")
+            d = stat[:, 0:n]
+            var = stat[:, WIDEST : WIDEST + n]
+            nc.tensor.matmul(d, center[:], x[:, 0:n], start=True, stop=True)
+            squares = norm.tile([CHANNELS, WIDEST], F32, name="squares")
+            nc.scalar.activation(squares[:, 0:n], d, ACT.Square)
+            nc.tensor.matmul(var, average[:], squares[:, 0:n], start=True, stop=True)
+            rstd = norm.tile([CHANNELS, WIDEST], F32, name="rstd")
+            nc.scalar.activation(rstd[:, 0:n], var, ACT.Abs_reciprocal_sqrt, bias=eps_col[:])
+            scaled = norm.tile([CHANNELS, WIDEST], F32, name="scaled")
+            nc.vector.tensor_tensor(scaled[:, 0:n], d, rstd[:, 0:n], ALU.mult)
+            nc.vector.tensor_scalar(y[:, j : j + n], scaled[:, 0:n], gain_col[:], beta_col[:], ALU.mult, ALU.add)
 
         def project(j, n):
             for b in range(BLOCKS):
@@ -98,8 +99,10 @@ def tile_main_kernel(tc, tok_emb, pos_emb, gain, beta, wl, bl, offs, out):
                     nc.vector.tensor_scalar_add(result[:, 0:n], logits[:, 0:n], bias[:, b : b + 1])
                 nc.sync.dma_start(out_by_block[:, b, j : j + n], result[:, 0:n])
 
-        for k in range(TOKENS // CHUNK):
-            normalise(k)
+        first_token = 0
+        for k, n in enumerate(CHUNKS):
+            normalise(k, first_token, n)
+            first_token += n
         first_token = 0
         for n in SPANS:
             project(first_token, n)

@@ -13,7 +13,7 @@ TOKENS = 1024
 EPS = 1e-5
 CHUNKS = (128, 128, 256, 256, 256)
 WIDEST = max(CHUNKS)
-SPANS = (128, 384, 512)
+SPANS = (256, 512, 256)
 BANK = 512
 BLOCKS = WORDS // 128
 

@@ -13,7 +13,7 @@ TOKENS = 1024
 EPS = 1e-5
 CHUNKS = (128, 128, 256, 256, 256)
 WIDEST = max(CHUNKS)
-SPANS = (256, 512, 256)
+SPANS = (256, 256, 512)
 BANK = 512
 BLOCKS = WORDS // 128
 
@@ -33,26 +33,27 @@ def tile_main_kernel(tc, tok_emb, pos_emb, gain, beta, wl, bl, offs, out):
         tc.psum_pool(name="stats", bufs=4) as stats,
         tc.psum_pool(name="banks", bufs=4) as banks,
     ):
-        offsets = held.tile([CHANNELS, TOKENS // 16], U16, name="offsets")
-        nc.sync.dma_start(offsets[:], offs)
         table = held.tile([CHANNELS, WORDS], F32, name="table")
         nc.sync.dma_start(table[:], tok_emb)
+        offsets = held.tile([CHANNELS, TOKENS // 16], U16, name="offsets")
+        nc.sync.dma_start(offsets[:], offs)
+        weights = held.tile([CHANNELS, WORDS], BF16, name="weights")
+        weights_by_block = weights[:].rearrange("c (p b) -> c b p", b=BLOCKS)
+        gain_col = held.tile([CHANNELS, 1], F32, name="gain_col")
+        beta_col = held.tile([CHANNELS, 1], F32, name="beta_col")
+        bias = held.tile([128, BLOCKS], F32, name="bias")
         positions = []
         first_token = 0
-        for n in CHUNKS:
+        for k, n in enumerate(CHUNKS):
             pos = norm.tile([CHANNELS, WIDEST], F32, name="pos")
             nc.sync.dma_start(pos[:, 0:n], pos_emb[:, first_token : first_token + n])
             positions.append(pos)
             first_token += n
-        weights = held.tile([CHANNELS, WORDS], BF16, name="weights")
-        weights_by_block = weights[:].rearrange("c (p b) -> c b p", b=BLOCKS)
-        gain_col = held.tile([CHANNELS, 1], F32, name="gain_col")
-        nc.scalar.dma_start(gain_col[:], gain)
-        beta_col = held.tile([CHANNELS, 1], F32, name="beta_col")
-        nc.scalar.dma_start(beta_col[:], beta)
-        bias = held.tile([128, BLOCKS], F32, name="bias")
-        nc.scalar.dma_start(bias[:], bl_by_block)
-        nc.scalar.dma_start(weights[:], wl)
+            if k == 2:
+                nc.sync.dma_start(gain_col[:], gain)
+                nc.sync.dma_start(beta_col[:], beta)
+                nc.sync.dma_start(weights[:], wl)
+                nc.sync.dma_start(bias[:], bl_by_block)
 
         identity = held.tile([CHANNELS, CHANNELS], F32, name="identity")
         make_identity(nc, identity[:])
@@ -99,11 +100,13 @@ def tile_main_kernel(tc, tok_emb, pos_emb, gain, beta, wl, bl, offs, out):
                     nc.vector.tensor_scalar_add(result[:, 0:n], logits[:, 0:n], bias[:, b : b + 1])
                 nc.sync.dma_start(out_by_block[:, b, j : j + n], result[:, 0:n])
 
-        first_token = 0
-        for k, n in enumerate(CHUNKS):
-            normalise(k, first_token, n)
-            first_token += n
-        first_token = 0
+        normalised = 0
+        projected = 0
+        k = 0
         for n in SPANS:
-            project(first_token, n)
-            first_token += n
+            while normalised < projected + n:
+                normalise(k, normalised, CHUNKS[k])
+                normalised += CHUNKS[k]
+                k += 1
+            project(projected, n)
+            projected += n

@@ -29,7 +29,7 @@ def tile_main_kernel(tc, tok_emb, pos_emb, gain, beta, wl, bl, offs, out):
         tc.tile_pool(name="held", bufs=1) as held,
         tc.tile_pool(name="norm", bufs=len(CHUNKS)) as norm,
         tc.tile_pool(name="summed", bufs=2) as summed,
-        tc.tile_pool(name="staged", bufs=len(SPANS) * BLOCKS) as staged,
+        tc.tile_pool(name="staged", bufs=BLOCKS) as staged,
         tc.psum_pool(name="stats", bufs=4) as stats,
         tc.psum_pool(name="banks", bufs=4) as banks,
     ):
@@ -90,15 +90,18 @@ def tile_main_kernel(tc, tok_emb, pos_emb, gain, beta, wl, bl, offs, out):
             nc.vector.tensor_scalar(y[:, j : j + n], scaled[:, 0:n], gain_col[:], beta_col[:], ALU.mult, ALU.add)
 
         def project(j, n):
-            for b in range(BLOCKS):
-                logits = banks.tile([128, BANK], F32, name="logits")
-                nc.tensor.matmul(logits[:, 0:n], weights_by_block[:, b, :], y[:, j : j + n], start=True, stop=True)
-                result = staged.tile([128, BANK], F32, name="result")
-                if b % 2 == 0:
-                    nc.scalar.activation(result[:, 0:n], logits[:, 0:n], ACT.Identity, bias=bias[:, b : b + 1])
-                else:
-                    nc.vector.tensor_scalar_add(result[:, 0:n], logits[:, 0:n], bias[:, b : b + 1])
-                nc.sync.dma_start(out_by_block[:, b, j : j + n], result[:, 0:n])
+            together = 1 if j == 0 else 2
+            for first in range(0, BLOCKS, together):
+                blocks = range(first, first + together)
+                result = staged.tile([128, together, n], F32, name="result", tag="result%d" % together)
+                for i, b in enumerate(blocks):
+                    logits = banks.tile([128, BANK], F32, name="logits")
+                    nc.tensor.matmul(logits[:, 0:n], weights_by_block[:, b, :], y[:, j : j + n], start=True, stop=True)
+                    if b % 2 == 0:
+                        nc.scalar.activation(result[:, i, :], logits[:, 0:n], ACT.Identity, bias=bias[:, b : b + 1])
+                    else:
+                        nc.vector.tensor_scalar_add(result[:, i, :], logits[:, 0:n], bias[:, b : b + 1])
+                nc.sync.dma_start(out_by_block[:, first : first + together, j : j + n], result[:])
 
         normalised = 0
         projected = 0

@@ -1,5 +1,4 @@
 import concourse.mybir as mybir
-from concourse.masks import make_identity
 
 F32 = mybir.dt.float32
 BF16 = mybir.dt.bfloat16
@@ -14,6 +13,7 @@ EPS = 1e-5
 CHUNKS = (128, 128, 256, 256, 256)
 WIDEST = max(CHUNKS)
 SPANS = (256, 256, 512)
+TOGETHER = (2, 4, 2)
 BANK = 512
 BLOCKS = WORDS // 128
 
@@ -29,7 +29,7 @@ def tile_main_kernel(tc, tok_emb, pos_emb, gain, beta, wl, bl, offs, out):
         tc.tile_pool(name="held", bufs=1) as held,
         tc.tile_pool(name="norm", bufs=len(CHUNKS)) as norm,
         tc.tile_pool(name="summed", bufs=2) as summed,
-        tc.tile_pool(name="staged", bufs=BLOCKS) as staged,
+        tc.tile_pool(name="staged", bufs=BLOCKS // min(TOGETHER)) as staged,
         tc.psum_pool(name="stats", bufs=4) as stats,
         tc.psum_pool(name="banks", bufs=4) as banks,
     ):
@@ -55,10 +55,17 @@ def tile_main_kernel(tc, tok_emb, pos_emb, gain, beta, wl, bl, offs, out):
                 nc.sync.dma_start(weights[:], wl)
                 nc.sync.dma_start(bias[:], bl_by_block)
 
-        identity = held.tile([CHANNELS, CHANNELS], F32, name="identity")
-        make_identity(nc, identity[:])
         center = held.tile([CHANNELS, CHANNELS], F32, name="center")
-        nc.vector.tensor_scalar_add(center[:], identity[:], -1.0 / CHANNELS)
+        nc.gpsimd.memset(center[:], -1.0 / CHANNELS)
+        nc.gpsimd.affine_select(
+            out=center[:],
+            in_=center[:],
+            pattern=[[-1, CHANNELS]],
+            compare_op=ALU.not_equal,
+            fill=1.0 - 1.0 / CHANNELS,
+            base=0,
+            channel_multiplier=1,
+        )
         average = held.tile([CHANNELS, CHANNELS], F32, name="average")
         nc.vector.memset(average[:], 1.0 / CHANNELS)
         eps_col = held.tile([CHANNELS, 1], F32, name="eps_col")
@@ -89,11 +96,10 @@ def tile_main_kernel(tc, tok_emb, pos_emb, gain, beta, wl, bl, offs, out):
             nc.vector.tensor_tensor(scaled[:, 0:n], d, rstd[:, 0:n], ALU.mult)
             nc.vector.tensor_scalar(y[:, j : j + n], scaled[:, 0:n], gain_col[:], beta_col[:], ALU.mult, ALU.add)
 
-        def project(j, n):
-            together = 1 if j == 0 else 2
+        def project(j, n, together):
             for first in range(0, BLOCKS, together):
                 blocks = range(first, first + together)
-                result = staged.tile([128, together, n], F32, name="result", tag="result%d" % together)
+                result = staged.tile([128, together, n], F32, name="result", tag="result%d" % j)
                 for i, b in enumerate(blocks):
                     logits = banks.tile([128, BANK], F32, name="logits")
                     nc.tensor.matmul(logits[:, 0:n], weights_by_block[:, b, :], y[:, j : j + n], start=True, stop=True)
@@ -106,10 +112,10 @@ def tile_main_kernel(tc, tok_emb, pos_emb, gain, beta, wl, bl, offs, out):
         normalised = 0
         projected = 0
         k = 0
-        for n in SPANS:
+        for n, together in zip(SPANS, TOGETHER):
             while normalised < projected + n:
                 normalise(k, normalised, CHUNKS[k])
                 normalised += CHUNKS[k]
                 k += 1
-            project(projected, n)
+            project(projected, n, together)
             projected += n

@@ -28,7 +28,7 @@ def tile_main_kernel(tc, tok_emb, pos_emb, gain, beta, wl, bl, offs, out):
     with (
         tc.tile_pool(name="held", bufs=1) as held,
         tc.tile_pool(name="norm", bufs=len(CHUNKS)) as norm,
-        tc.tile_pool(name="summed", bufs=2) as summed,
+        tc.tile_pool(name="summed", bufs=len(CHUNKS)) as summed,
         tc.tile_pool(name="staged", bufs=BLOCKS // min(TOGETHER)) as staged,
         tc.psum_pool(name="stats", bufs=4) as stats,
         tc.psum_pool(name="banks", bufs=4) as banks,
@@ -73,7 +73,7 @@ def tile_main_kernel(tc, tok_emb, pos_emb, gain, beta, wl, bl, offs, out):
         primed = held.tile([CHANNELS, 1], F32, name="primed")
         nc.scalar.activation(primed[:], eps_col[:], ACT.Abs_reciprocal_sqrt)
 
-        for i in range(8):
+        for i in range(6):
             idle = banks.tile([CHANNELS, CHANNELS], F32, name="logits")
             nc.tensor.matmul(idle[:], average[:], average[:], start=True, stop=True)
 

@@ -109,13 +109,12 @@ def tile_main_kernel(tc, tok_emb, pos_emb, gain, beta, wl, bl, offs, out):
                         nc.vector.tensor_scalar_add(result[:, i, :], logits[:, 0:n], bias[:, b : b + 1])
                 nc.sync.dma_start(out_by_block[:, first : first + together, j : j + n], result[:])
 
-        normalised = 0
-        projected = 0
-        k = 0
-        for n, together in zip(SPANS, TOGETHER):
-            while normalised < projected + n:
-                normalise(k, normalised, CHUNKS[k])
-                normalised += CHUNKS[k]
-                k += 1
+        starts = [sum(CHUNKS[:k]) for k in range(len(CHUNKS))]
+        for k, n in enumerate(CHUNKS):
+            normalise(k, starts[k], n)
+            if starts[k] + n == SPANS[0]:
+                project(0, SPANS[0], TOGETHER[0])
+        projected = SPANS[0]
+        for n, together in zip(SPANS[1:], TOGETHER[1:]):
             project(projected, n, together)
             projected += n

import concourse.mybir as mybir

F32 = mybir.dt.float32
BF16 = mybir.dt.bfloat16
U16 = mybir.dt.uint16
ALU = mybir.AluOpType
ACT = mybir.ActivationFunctionType

CHANNELS = 128
WORDS = 1024
TOKENS = 1024
EPS = 1e-5
CHUNKS = (128, 128, 256, 256, 256)
WIDEST = max(CHUNKS)
SPANS = (256, 256, 512)
TOGETHER = (2, 4, 2)
BANK = 512
BLOCKS = WORDS // 128

FLOPS = 2 * CHANNELS * WORDS * TOKENS


def tile_main_kernel(tc, tok_emb, pos_emb, gain, beta, wl, bl, offs, out):
    nc = tc.nc
    bl_by_block = bl.rearrange("(p b) o -> p (b o)", b=BLOCKS)
    out_by_block = out.rearrange("(p b) j -> p b j", b=BLOCKS)

    with (
        tc.tile_pool(name="held", bufs=1) as held,
        tc.tile_pool(name="norm", bufs=len(CHUNKS)) as norm,
        tc.tile_pool(name="summed", bufs=len(CHUNKS)) as summed,
        tc.tile_pool(name="staged", bufs=BLOCKS // min(TOGETHER)) as staged,
        tc.psum_pool(name="stats", bufs=4) as stats,
        tc.psum_pool(name="banks", bufs=4) as banks,
    ):
        table = held.tile([CHANNELS, WORDS], F32, name="table")
        nc.sync.dma_start(table[:], tok_emb)
        offsets = held.tile([CHANNELS, TOKENS // 16], U16, name="offsets")
        nc.sync.dma_start(offsets[:], offs)
        weights = held.tile([CHANNELS, WORDS], BF16, name="weights")
        weights_by_block = weights[:].rearrange("c (p b) -> c b p", b=BLOCKS)
        gain_col = held.tile([CHANNELS, 1], F32, name="gain_col")
        beta_col = held.tile([CHANNELS, 1], F32, name="beta_col")
        bias = held.tile([128, BLOCKS], F32, name="bias")
        positions = []
        first_token = 0
        for k, n in enumerate(CHUNKS):
            pos = norm.tile([CHANNELS, WIDEST], F32, name="pos")
            nc.sync.dma_start(pos[:, 0:n], pos_emb[:, first_token : first_token + n])
            positions.append(pos)
            first_token += n
            if k == 2:
                nc.sync.dma_start(gain_col[:], gain)
                nc.sync.dma_start(beta_col[:], beta)
                nc.sync.dma_start(weights[:], wl)
                nc.sync.dma_start(bias[:], bl_by_block)

        center = held.tile([CHANNELS, CHANNELS], F32, name="center")
        nc.gpsimd.memset(center[:], -1.0 / CHANNELS)
        nc.gpsimd.affine_select(
            out=center[:],
            in_=center[:],
            pattern=[[-1, CHANNELS]],
            compare_op=ALU.not_equal,
            fill=1.0 - 1.0 / CHANNELS,
            base=0,
            channel_multiplier=1,
        )
        average = held.tile([CHANNELS, CHANNELS], F32, name="average")
        nc.vector.memset(average[:], 1.0 / CHANNELS)
        eps_col = held.tile([CHANNELS, 1], F32, name="eps_col")
        nc.vector.memset(eps_col[:], EPS)
        primed = held.tile([CHANNELS, 1], F32, name="primed")
        nc.scalar.activation(primed[:], eps_col[:], ACT.Abs_reciprocal_sqrt)

        for i in range(6):
            idle = banks.tile([CHANNELS, CHANNELS], F32, name="logits")
            nc.tensor.matmul(idle[:], average[:], average[:], start=True, stop=True)

        y = held.tile([CHANNELS, TOKENS], BF16, name="y")

        def normalise(k, j, n):
            piece = offsets[:, j // 16 : (j + n) // 16]
            x = summed.tile([CHANNELS, WIDEST], F32, name="x")
            nc.vector.tensor_tensor(x[:, 0:n], table[:].indirect(piece), positions[k][:, 0:n], ALU.add)
            stat = stats.tile([CHANNELS, 2 * WIDEST], F32, name="stat")
            d = stat[:, 0:n]
            var = stat[:, WIDEST : WIDEST + n]
            nc.tensor.matmul(d, center[:], x[:, 0:n], start=True, stop=True)
            squares = norm.tile([CHANNELS, WIDEST], F32, name="squares")
            nc.scalar.activation(squares[:, 0:n], d, ACT.Square)
            nc.tensor.matmul(var, average[:], squares[:, 0:n], start=True, stop=True)
            rstd = norm.tile([CHANNELS, WIDEST], F32, name="rstd")
            nc.scalar.activation(rstd[:, 0:n], var, ACT.Abs_reciprocal_sqrt, bias=eps_col[:])
            scaled = norm.tile([CHANNELS, WIDEST], F32, name="scaled")
            nc.vector.tensor_tensor(scaled[:, 0:n], d, rstd[:, 0:n], ALU.mult)
            nc.vector.tensor_scalar(y[:, j : j + n], scaled[:, 0:n], gain_col[:], beta_col[:], ALU.mult, ALU.add)

        def project(j, n, together):
            for first in range(0, BLOCKS, together):
                blocks = range(first, first + together)
                result = staged.tile([128, together, n], F32, name="result", tag="result%d" % j)
                for i, b in enumerate(blocks):
                    logits = banks.tile([128, BANK], F32, name="logits")
                    nc.tensor.matmul(logits[:, 0:n], weights_by_block[:, b, :], y[:, j : j + n], start=True, stop=True)
                    if b % 2 == 0:
                        nc.scalar.activation(result[:, i, :], logits[:, 0:n], ACT.Identity, bias=bias[:, b : b + 1])
                    else:
                        nc.vector.tensor_scalar_add(result[:, i, :], logits[:, 0:n], bias[:, b : b + 1])
                nc.sync.dma_start(out_by_block[:, first : first + together, j : j + n], result[:])

        starts = [sum(CHUNKS[:k]) for k in range(len(CHUNKS))]
        for k, n in enumerate(CHUNKS):
            normalise(k, starts[k], n)
            if starts[k] + n == SPANS[0]:
                project(0, SPANS[0], TOGETHER[0])
        projected = SPANS[0]
        for n, together in zip(SPANS[1:], TOGETHER[1:]):
            project(projected, n, together)
            projected += n
